import numpy as np
import ml_dtypes


def mxq(x, axis, fmt="e4m3"):
    dtype, down = {"e4m3": (ml_dtypes.float8_e4m3fn, 7), "e5m2": (ml_dtypes.float8_e5m2, 14)}[fmt]
    v = np.moveaxis(np.asarray(x, np.float32).astype(ml_dtypes.bfloat16).astype(np.float64), axis, -1)
    blocks = v.reshape(v.shape[:-1] + (-1, 32))
    amax = np.abs(blocks).max(-1, keepdims=True)
    byte = np.maximum(np.where(amax > 0, np.frexp(amax)[1] - 1 + 127, 0) - down, 1)
    scale = np.exp2(byte - 127.0)
    codes = (blocks / scale).astype(np.float32).astype(dtype).astype(np.float64)
    return np.moveaxis((codes * scale).reshape(v.shape), -1, axis)


WIDE = False


def mx_kscale(k):
    if not WIDE:
        return np.ones(k)
    levels = np.array([10, -10, 5, -5, 0])
    a = np.random.permutation(np.resize(levels, k // 512 * 4)).reshape(k // 512, 4)
    idx = np.arange(k)
    return np.exp2(a[idx // 512, idx % 128 // 32])


BF16 = ml_dtypes.bfloat16


def bf(x):
    return np.asarray(x, np.float32).astype(BF16)


def f64(x):
    return np.asarray(x).astype(np.float64)


B, G, Z1, Z2, H, PD = 4096, 2, 256, 256, 512, 512
CIN = Z1 + Z2


def glin(x, W, b):
    y = mxq(x, 2, "e4m3").transpose(1, 0, 2) @ mxq(f64(W), 2, "e4m3").transpose(0, 2, 1)
    return y.transpose(1, 0, 2) + f64(b)


def setup_inputs():
    s = mx_kscale(CIN)
    return {"z1": bf((np.random.standard_normal((B, G, Z1)) * s[:Z1]).reshape(B, G * Z1)),
            "z2": bf((np.random.standard_normal((B, G, Z2)) * s[Z1:]).reshape(B, G * Z2)),
            "W1": bf(np.random.standard_normal((G, H, CIN)) / np.sqrt(CIN) / s),
            "b1": bf(np.random.standard_normal((G, H)) * 0.2),
            "W2": bf(np.random.standard_normal((G, H, H)) * 1.4 / np.sqrt(H)),
            "b2": bf(np.random.standard_normal((G, H)) * 0.2)}


def reference(z1, z2, W1, b1, W2, b2):
    z = np.concatenate([f64(z1).reshape(B, G, Z1), f64(z2).reshape(B, G, Z2)], axis=2)
    h1 = np.maximum(glin(z, W1, b1), 0.0)
    return np.maximum(glin(h1, W2, b2), 0.0) + h1

@@ -1,0 +1,196 @@
+from contextlib import ExitStack
+
+import concourse.mybir as mybir
+from concourse.masks import make_identity
+
+F32 = mybir.dt.float32
+BF16 = mybir.dt.bfloat16
+U32 = mybir.dt.uint32
+U8 = mybir.dt.uint8
+FP8X4 = mybir.dt.float8_e4m3fn_x4
+ADD = mybir.AluOpType.add
+MAX = mybir.AluOpType.max
+RELU = mybir.ActivationFunctionType.Relu
+
+P = 128
+PACK = 4
+BATCH = 4096
+CODES = 2
+Z_HALF = 256
+HIDDEN = 512
+ROWS = 512
+SUB = ROWS // P
+CHUNKS = BATCH // ROWS
+SCALAR_SHARE = 3
+
+FLOPS = 2 * BATCH * CODES * (2 * Z_HALF * HIDDEN + HIDDEN * HIDDEN)
+
+
+def words_onto_partitions(nc, psum, ident, blocks, grouped_words, copy):
+    flipped = psum.tile([P, 2, 2 * P], F32, tag="flipped")
+    for n, halves in enumerate(blocks):
+        for u, words in enumerate(halves):
+            nc.tensor.transpose(flipped[:, u, n * P : (n + 1) * P], words, ident[:])
+    copy(out=grouped_words, in_=flipped[:].rearrange("q u c -> q c u"))
+
+
+def tile_linearwdecoder_pa_t_kernel(tc, z1, z2, W1, b1, W2, b2, out):
+    nc = tc.nc
+    with ExitStack() as ctx:
+        const = ctx.enter_context(tc.tile_pool(name="const", bufs=1))
+        inputs = ctx.enter_context(tc.tile_pool(name="inputs", bufs=1))
+        work = ctx.enter_context(tc.tile_pool(name="work", bufs=3))
+        psum = ctx.enter_context(tc.psum_pool(name="psum", bufs=2))
+
+        ident_f32 = const.tile([P, P], F32)
+        make_identity(nc, ident_f32[:])
+        ident_bf16 = const.tile([P, P], BF16)
+        make_identity(nc, ident_bf16[:])
+
+        w1_raw = []
+        w2_raw = []
+        z_raw = []
+        for g in range(CODES):
+            w1_g = inputs.tile([P, PACK, HIDDEN], BF16, name="w1_raw_%d" % g)
+            w1_raw.append(w1_g)
+            w2_g = inputs.tile([P, PACK, HIDDEN], BF16, name="w2_raw_%d" % g)
+            w2_raw.append(w2_g)
+        for c in range(CHUNKS):
+            z1_c = inputs.tile([P, SUB, CODES * Z_HALF], BF16, name="z1_raw_%d" % c)
+            z2_c = inputs.tile([P, SUB, CODES * Z_HALF], BF16, name="z2_raw_%d" % c)
+            z_raw.append((z1_c, z2_c))
+
+        def load_z(c):
+            rows = slice(c * ROWS, (c + 1) * ROWS)
+            nc.sync.dma_start(out=z_raw[c][0][:], in_=z1[rows, :].rearrange("(p j) k -> p j k", j=SUB))
+            nc.sync.dma_start(out=z_raw[c][1][:], in_=z2[rows, :].rearrange("(p j) k -> p j k", j=SUB))
+
+        bias_rows = const.tile([P, P], BF16)
+        nc.vector.memset(bias_rows[:], 0.0)
+        b2_bf16 = const.tile([P, CODES * HIDDEN], BF16)
+
+        nc.sync.dma_start(out=w1_raw[0][:], in_=W1[0].rearrange("(a p) k -> p a k", p=P))
+        load_z(0)
+        nc.sync.dma_start(out=bias_rows[0 : CODES * PACK, :], in_=b1.rearrange("g (a p) -> (g a) p", p=P))
+        nc.sync.dma_start(out=w1_raw[1][:], in_=W1[1].rearrange("(a p) k -> p a k", p=P))
+        nc.sync.dma_start(out=w2_raw[0][:], in_=W2[0].rearrange("(a p) k -> p a k", p=P))
+        nc.sync.dma_start(out=w2_raw[1][:], in_=W2[1].rearrange("(a p) k -> p a k", p=P))
+        nc.sync.dma_start(out=b2_bf16[:], in_=b2.rearrange("g n -> (g n)").partition_broadcast(P))
+        for c in range(1, CHUNKS):
+            load_z(c)
+
+        bias_flipped = psum.tile([P, P], BF16, tag="back")
+        nc.tensor.transpose(bias_flipped[:], bias_rows[:], ident_bf16[:])
+        b1_col = const.tile([P, CODES * PACK], F32)
+        nc.vector.tensor_copy(out=b1_col[:], in_=bias_flipped[:, 0 : CODES * PACK])
+        b2_all = const.tile([P, CODES, HIDDEN], F32)
+        nc.vector.tensor_copy(out=b2_all[:].rearrange("p g n -> p (g n)"), in_=b2_bf16[:])
+
+        w1_codes = const.tile([P, CODES, HIDDEN], U32, align_bytes=64)
+        w1_scales = const.tile([P, CODES, HIDDEN], U8, align_bytes=64)
+        w2_codes = const.tile([P, CODES, HIDDEN], U32, align_bytes=64)
+        w2_scales = const.tile([P, CODES, HIDDEN], U8, align_bytes=64)
+        for g in range(CODES):
+            w1_grouped = work.tile([P, HIDDEN * PACK], BF16, tag="w_grouped", align_bytes=64)
+            w1_words = w1_grouped[:].bitcast(F32).rearrange("q (c u) -> q c u", u=2)
+            for h in range(2):
+                blocks = []
+                for a in (2 * h, 2 * h + 1):
+                    words = w1_raw[g][:, a, :].bitcast(F32)
+                    blocks.append((words[:, 0:P], words[:, P : 2 * P]))
+                words_onto_partitions(
+                    nc, psum, ident_f32, blocks, w1_words[:, h * 2 * P : (h + 1) * 2 * P, :], nc.vector.tensor_copy
+                )
+            nc.vector.quantize_mx(out=w1_codes[:, g, :].bitcast(FP8X4), scales=w1_scales[:, g, :], in_=w1_grouped[:])
+        for g in range(CODES):
+            w2_grouped = work.tile([P, HIDDEN, PACK], BF16, tag="w_grouped", align_bytes=64)
+            for a in range(PACK):
+                w2_flipped = psum.tile([P, PACK, P], BF16, tag="back")
+                for t in range(PACK):
+                    nc.tensor.transpose(w2_flipped[:, t, :], w2_raw[g][:, a, t * P : (t + 1) * P], ident_bf16[:])
+                nc.scalar.copy(
+                    out=w2_grouped[:, a * P : (a + 1) * P, :], in_=w2_flipped[:].rearrange("k t c -> k c t")
+                )
+            nc.vector.quantize_mx(
+                out=w2_codes[:, g, :].bitcast(FP8X4),
+                scales=w2_scales[:, g, :],
+                in_=w2_grouped[:].rearrange("k c t -> k (c t)"),
+            )
+
+        for c in range(CHUNKS):
+            for g in range(CODES):
+                z_grouped = work.tile([P, ROWS * PACK], BF16, align_bytes=64)
+                z_words = z_grouped[:].bitcast(F32).rearrange("q (c u) -> q c u", u=2)
+                for h in range(2):
+                    blocks = []
+                    for j in (2 * h, 2 * h + 1):
+                        blocks.append(
+                            (
+                                z_raw[c][0][:, j, :].bitcast(F32)[:, g * P : (g + 1) * P],
+                                z_raw[c][1][:, j, :].bitcast(F32)[:, g * P : (g + 1) * P],
+                            )
+                        )
+                    words_onto_partitions(
+                        nc, psum, ident_f32, blocks, z_words[:, h * 2 * P : (h + 1) * 2 * P, :], nc.scalar.copy
+                    )
+                z_codes = work.tile([P, ROWS], U32, align_bytes=64)
+                z_scales = work.tile([P, ROWS], U8, align_bytes=64)
+                nc.vector.quantize_mx(out=z_codes[:].bitcast(FP8X4), scales=z_scales[:], in_=z_grouped[:])
+
+                hidden = work.tile([P, PACK, ROWS], F32, bufs=4)
+                for t in range(PACK):
+                    s1 = psum.tile([P, ROWS], F32, tag="s1")
+                    nc.tensor.matmul_mx(
+                        out=s1[:],
+                        lhsT=w1_codes[:, g, t * P : (t + 1) * P].bitcast(FP8X4),
+                        lhsT_scale=w1_scales[:, g, t * P : (t + 1) * P],
+                        rhs=z_codes[:].bitcast(FP8X4),
+                        rhs_scale=z_scales[:],
+                        start=True,
+                        stop=True,
+                    )
+                    nc.scalar.activation(
+                        out=hidden[:, t, :],
+                        in_=s1[:],
+                        func=RELU,
+                        bias=b1_col[:, g * PACK + t : g * PACK + t + 1],
+                        scale=1.0,
+                    )
+
+                h_grouped = work.tile([P, ROWS, PACK], BF16, align_bytes=64)
+                for j in range(SUB):
+                    cols = slice(j * P, (j + 1) * P)
+                    planes = hidden[:, :, cols].rearrange("p t b -> p b t")
+                    if j < SCALAR_SHARE:
+                        nc.scalar.copy(out=h_grouped[:, cols, :], in_=planes)
+                    else:
+                        nc.vector.tensor_copy(out=h_grouped[:, cols, :], in_=planes)
+                h_codes = work.tile([P, ROWS], U32, align_bytes=64)
+                h_scales = work.tile([P, ROWS], U8, align_bytes=64)
+                nc.vector.quantize_mx(
+                    out=h_codes[:].bitcast(FP8X4), scales=h_scales[:], in_=h_grouped[:].rearrange("p b t -> p (b t)")
+                )
+
+                result = work.tile([P, SUB, HIDDEN], F32)
+                for j in range(SUB):
+                    cols = slice(j * P, (j + 1) * P)
+                    back = psum.tile([P, HIDDEN], F32, tag="back")
+                    for t in range(PACK):
+                        nc.tensor.transpose(back[:, t * P : (t + 1) * P], hidden[:, t, cols], ident_f32[:])
+                    s2 = psum.tile([P, HIDDEN], F32, tag="s2")
+                    nc.tensor.matmul_mx(
+                        out=s2[:],
+                        lhsT=h_codes[:, cols].bitcast(FP8X4),
+                        lhsT_scale=h_scales[:, cols],
+                        rhs=w2_codes[:, g, :].bitcast(FP8X4),
+                        rhs_scale=w2_scales[:, g, :],
+                        start=True,
+                        stop=True,
+                    )
+                    pre = work.tile([P, HIDDEN], F32, bufs=4)
+                    nc.vector.tensor_tensor(out=pre[:], in0=s2[:], in1=b2_all[:, g, :], op=ADD)
+                    nc.vector.scalar_tensor_tensor(
+                        out=result[:, j, :], in0=pre[:], scalar=0.0, in1=back[:], op0=MAX, op1=ADD
+                    )
+                rows = slice(c * ROWS, (c + 1) * ROWS)
+                nc.sync.dma_start(out=out[rows, g, :].rearrange("(p j) n -> p j n", j=SUB), in_=result[:])

@@ -21,17 +21,10 @@ HIDDEN = 512
 ROWS = 512
 SUB = ROWS // P
 CHUNKS = BATCH // ROWS
+UNITS = CHUNKS * CODES
 SCALAR_SHARE = 3
 
 FLOPS = 2 * BATCH * CODES * (2 * Z_HALF * HIDDEN + HIDDEN * HIDDEN)
-
-
-def words_onto_partitions(nc, psum, ident, blocks, grouped_words, copy):
-    flipped = psum.tile([P, 2, 2 * P], F32, tag="flipped")
-    for n, halves in enumerate(blocks):
-        for u, words in enumerate(halves):
-            nc.tensor.transpose(flipped[:, u, n * P : (n + 1) * P], words, ident[:])
-    copy(out=grouped_words, in_=flipped[:].rearrange("q u c -> q c u"))
 
 
 def tile_linearwdecoder_pa_t_kernel(tc, z1, z2, W1, b1, W2, b2, out):
@@ -39,8 +32,9 @@ def tile_linearwdecoder_pa_t_kernel(tc, z1, z2, W1, b1, W2, b2, out):
     with ExitStack() as ctx:
         const = ctx.enter_context(tc.tile_pool(name="const", bufs=1))
         inputs = ctx.enter_context(tc.tile_pool(name="inputs", bufs=1))
-        work = ctx.enter_context(tc.tile_pool(name="work", bufs=3))
+        work = ctx.enter_context(tc.tile_pool(name="work", bufs=2))
         psum = ctx.enter_context(tc.psum_pool(name="psum", bufs=2))
+        ctx.enter_context(tc.manual_schedule())
 
         ident_f32 = const.tile([P, P], F32)
         make_identity(nc, ident_f32[:])
@@ -65,32 +59,44 @@ def tile_linearwdecoder_pa_t_kernel(tc, z1, z2, W1, b1, W2, b2, out):
             nc.sync.dma_start(out=z_raw[c][0][:], in_=z1[rows, :].rearrange("(p j) k -> p j k", j=SUB))
             nc.sync.dma_start(out=z_raw[c][1][:], in_=z2[rows, :].rearrange("(p j) k -> p j k", j=SUB))
 
+        def load_w(raw, w, g):
+            nc.sync.dma_start(out=raw[g][:], in_=w[g].rearrange("(a p) k -> p a k", p=P))
+
         bias_rows = const.tile([P, P], BF16)
         nc.vector.memset(bias_rows[:], 0.0)
         b2_bf16 = const.tile([P, CODES * HIDDEN], BF16)
 
-        nc.sync.dma_start(out=w1_raw[0][:], in_=W1[0].rearrange("(a p) k -> p a k", p=P))
         load_z(0)
+        load_w(w1_raw, W1, 0)
         nc.sync.dma_start(out=bias_rows[0 : CODES * PACK, :], in_=b1.rearrange("g (a p) -> (g a) p", p=P))
-        nc.sync.dma_start(out=w1_raw[1][:], in_=W1[1].rearrange("(a p) k -> p a k", p=P))
-        nc.sync.dma_start(out=w2_raw[0][:], in_=W2[0].rearrange("(a p) k -> p a k", p=P))
-        nc.sync.dma_start(out=w2_raw[1][:], in_=W2[1].rearrange("(a p) k -> p a k", p=P))
+        load_w(w2_raw, W2, 0)
+        load_w(w1_raw, W1, 1)
+        load_w(w2_raw, W2, 1)
         nc.sync.dma_start(out=b2_bf16[:], in_=b2.rearrange("g n -> (g n)").partition_broadcast(P))
         for c in range(1, CHUNKS):
             load_z(c)
-
-        bias_flipped = psum.tile([P, P], BF16, tag="back")
-        nc.tensor.transpose(bias_flipped[:], bias_rows[:], ident_bf16[:])
-        b1_col = const.tile([P, CODES * PACK], F32)
-        nc.vector.tensor_copy(out=b1_col[:], in_=bias_flipped[:, 0 : CODES * PACK])
-        b2_all = const.tile([P, CODES, HIDDEN], F32)
-        nc.vector.tensor_copy(out=b2_all[:].rearrange("p g n -> p (g n)"), in_=b2_bf16[:])
 
         w1_codes = const.tile([P, CODES, HIDDEN], U32, align_bytes=64)
         w1_scales = const.tile([P, CODES, HIDDEN], U8, align_bytes=64)
         w2_codes = const.tile([P, CODES, HIDDEN], U32, align_bytes=64)
         w2_scales = const.tile([P, CODES, HIDDEN], U8, align_bytes=64)
-        for g in range(CODES):
+        b1_col = const.tile([P, CODES * PACK], F32)
+        b2_all = const.tile([P, CODES, HIDDEN], F32)
+
+        def words_onto_partitions(blocks, grouped_words, copy):
+            flipped = psum.tile([P, 2, 2 * P], F32, tag="flipped")
+            for n, halves in enumerate(blocks):
+                for u, words in enumerate(halves):
+                    nc.tensor.transpose(flipped[:, u, n * P : (n + 1) * P], words, ident_f32[:])
+            copy(out=grouped_words, in_=flipped[:].rearrange("q u c -> q c u"))
+
+        def prepare_biases():
+            bias_flipped = psum.tile([P, P], BF16, tag="back")
+            nc.tensor.transpose(bias_flipped[:], bias_rows[:], ident_bf16[:])
+            nc.vector.tensor_copy(out=b1_col[:], in_=bias_flipped[:, 0 : CODES * PACK])
+            nc.gpsimd.tensor_copy(out=b2_all[:].rearrange("p g n -> p (g n)"), in_=b2_bf16[:])
+
+        def prepare_w1(g):
             w1_grouped = work.tile([P, HIDDEN * PACK], BF16, tag="w_grouped", align_bytes=64)
             w1_words = w1_grouped[:].bitcast(F32).rearrange("q (c u) -> q c u", u=2)
             for h in range(2):
@@ -98,99 +104,199 @@ def tile_linearwdecoder_pa_t_kernel(tc, z1, z2, W1, b1, W2, b2, out):
                 for a in (2 * h, 2 * h + 1):
                     words = w1_raw[g][:, a, :].bitcast(F32)
                     blocks.append((words[:, 0:P], words[:, P : 2 * P]))
-                words_onto_partitions(
-                    nc, psum, ident_f32, blocks, w1_words[:, h * 2 * P : (h + 1) * 2 * P, :], nc.vector.tensor_copy
-                )
+                words_onto_partitions(blocks, w1_words[:, h * 2 * P : (h + 1) * 2 * P, :], nc.vector.tensor_copy)
             nc.vector.quantize_mx(out=w1_codes[:, g, :].bitcast(FP8X4), scales=w1_scales[:, g, :], in_=w1_grouped[:])
-        for g in range(CODES):
+
+        def prepare_w2(g, copy):
             w2_grouped = work.tile([P, HIDDEN, PACK], BF16, tag="w_grouped", align_bytes=64)
             for a in range(PACK):
                 w2_flipped = psum.tile([P, PACK, P], BF16, tag="back")
                 for t in range(PACK):
                     nc.tensor.transpose(w2_flipped[:, t, :], w2_raw[g][:, a, t * P : (t + 1) * P], ident_bf16[:])
-                nc.scalar.copy(
-                    out=w2_grouped[:, a * P : (a + 1) * P, :], in_=w2_flipped[:].rearrange("k t c -> k c t")
-                )
+                copy(out=w2_grouped[:, a * P : (a + 1) * P, :], in_=w2_flipped[:].rearrange("k t c -> k c t"))
             nc.vector.quantize_mx(
                 out=w2_codes[:, g, :].bitcast(FP8X4),
                 scales=w2_scales[:, g, :],
                 in_=w2_grouped[:].rearrange("k c t -> k (c t)"),
             )
 
-        for c in range(CHUNKS):
-            for g in range(CODES):
-                z_grouped = work.tile([P, ROWS * PACK], BF16, align_bytes=64)
-                z_words = z_grouped[:].bitcast(F32).rearrange("q (c u) -> q c u", u=2)
-                for h in range(2):
-                    blocks = []
-                    for j in (2 * h, 2 * h + 1):
-                        blocks.append(
-                            (
-                                z_raw[c][0][:, j, :].bitcast(F32)[:, g * P : (g + 1) * P],
-                                z_raw[c][1][:, j, :].bitcast(F32)[:, g * P : (g + 1) * P],
-                            )
-                        )
-                    words_onto_partitions(
-                        nc, psum, ident_f32, blocks, z_words[:, h * 2 * P : (h + 1) * 2 * P, :], nc.scalar.copy
-                    )
-                z_codes = work.tile([P, ROWS], U32, align_bytes=64)
-                z_scales = work.tile([P, ROWS], U8, align_bytes=64)
-                nc.vector.quantize_mx(out=z_codes[:].bitcast(FP8X4), scales=z_scales[:], in_=z_grouped[:])
+        z_grouped = {}
+        z_codes = {}
+        hidden = {}
+        h_grouped = {}
+        h_codes = {}
+        back = {}
+        s2 = {}
+        pre = {}
 
-                hidden = work.tile([P, PACK, ROWS], F32, bufs=4)
-                for t in range(PACK):
-                    s1 = psum.tile([P, ROWS], F32, tag="s1")
-                    nc.tensor.matmul_mx(
-                        out=s1[:],
-                        lhsT=w1_codes[:, g, t * P : (t + 1) * P].bitcast(FP8X4),
-                        lhsT_scale=w1_scales[:, g, t * P : (t + 1) * P],
-                        rhs=z_codes[:].bitcast(FP8X4),
-                        rhs_scale=z_scales[:],
-                        start=True,
-                        stop=True,
-                    )
-                    nc.scalar.activation(
-                        out=hidden[:, t, :],
-                        in_=s1[:],
-                        func=RELU,
-                        bias=b1_col[:, g * PACK + t : g * PACK + t + 1],
-                        scale=1.0,
-                    )
+        def exists(u):
+            return 0 <= u < UNITS
 
-                h_grouped = work.tile([P, ROWS, PACK], BF16, align_bytes=64)
-                for j in range(SUB):
-                    cols = slice(j * P, (j + 1) * P)
-                    planes = hidden[:, :, cols].rearrange("p t b -> p b t")
-                    if j < SCALAR_SHARE:
-                        nc.scalar.copy(out=h_grouped[:, cols, :], in_=planes)
-                    else:
-                        nc.vector.tensor_copy(out=h_grouped[:, cols, :], in_=planes)
-                h_codes = work.tile([P, ROWS], U32, align_bytes=64)
-                h_scales = work.tile([P, ROWS], U8, align_bytes=64)
-                nc.vector.quantize_mx(
-                    out=h_codes[:].bitcast(FP8X4), scales=h_scales[:], in_=h_grouped[:].rearrange("p b t -> p (b t)")
+        def transpose_z(u, h):
+            if not exists(u):
+                return
+            if h == 0:
+                grouped = work.tile([P, ROWS * PACK], BF16, tag="z_grouped", bufs=3, align_bytes=64)
+                z_grouped[u] = grouped
+            c, g = divmod(u, CODES)
+            z_words = z_grouped[u][:].bitcast(F32).rearrange("q (c u) -> q c u", u=2)
+            blocks = []
+            for j in (2 * h, 2 * h + 1):
+                blocks.append(
+                    (
+                        z_raw[c][0][:, j, :].bitcast(F32)[:, g * P : (g + 1) * P],
+                        z_raw[c][1][:, j, :].bitcast(F32)[:, g * P : (g + 1) * P],
+                    )
+                )
+            words_onto_partitions(blocks, z_words[:, h * 2 * P : (h + 1) * 2 * P, :], nc.scalar.copy)
+
+        def quantise_z(u):
+            if not exists(u):
+                return
+            codes = work.tile([P, ROWS], U32, tag="z_codes", align_bytes=64)
+            scales = work.tile([P, ROWS], U8, tag="z_scales", align_bytes=64)
+            z_codes[u] = (codes, scales)
+            nc.vector.quantize_mx(out=codes[:].bitcast(FP8X4), scales=scales[:], in_=z_grouped[u][:])
+
+        def layer1(u, t):
+            if not exists(u):
+                return
+            if t == 0:
+                planes = work.tile([P, PACK, ROWS], F32, tag="hidden", bufs=4)
+                hidden[u] = planes
+            g = u % CODES
+            codes, scales = z_codes[u]
+            s1 = psum.tile([P, ROWS], F32, tag="s1")
+            nc.tensor.matmul_mx(
+                out=s1[:],
+                lhsT=w1_codes[:, g, t * P : (t + 1) * P].bitcast(FP8X4),
+                lhsT_scale=w1_scales[:, g, t * P : (t + 1) * P],
+                rhs=codes[:].bitcast(FP8X4),
+                rhs_scale=scales[:],
+                start=True,
+                stop=True,
+            )
+            nc.scalar.activation(
+                out=hidden[u][:, t, :],
+                in_=s1[:],
+                func=RELU,
+                bias=b1_col[:, g * PACK + t : g * PACK + t + 1],
+                scale=1.0,
+            )
+
+        def regroup_h(u):
+            if not exists(u):
+                return
+            grouped = work.tile([P, ROWS, PACK], BF16, tag="h_grouped", align_bytes=64)
+            h_grouped[u] = grouped
+            for j in range(SUB):
+                cols = slice(j * P, (j + 1) * P)
+                planes = hidden[u][:, :, cols].rearrange("p t b -> p b t")
+                if j < SCALAR_SHARE:
+                    nc.scalar.copy(out=grouped[:, cols, :], in_=planes)
+                else:
+                    nc.vector.tensor_copy(out=grouped[:, cols, :], in_=planes)
+
+        def quantise_h(u):
+            if not exists(u):
+                return
+            codes = work.tile([P, ROWS], U32, tag="h_codes", align_bytes=64)
+            scales = work.tile([P, ROWS], U8, tag="h_scales", align_bytes=64)
+            h_codes[u] = (codes, scales)
+            nc.vector.quantize_mx(
+                out=codes[:].bitcast(FP8X4), scales=scales[:], in_=h_grouped[u][:].rearrange("p b t -> p (b t)")
+            )
+
+        def residual_back(u, j):
+            if not exists(u):
+                return
+            rows_first = psum.tile([P, HIDDEN], F32, tag="back")
+            back[(u, j)] = rows_first
+            for t in range(PACK):
+                nc.tensor.transpose(
+                    rows_first[:, t * P : (t + 1) * P], hidden[u][:, t, j * P : (j + 1) * P], ident_f32[:]
                 )
 
-                result = work.tile([P, SUB, HIDDEN], F32)
-                for j in range(SUB):
-                    cols = slice(j * P, (j + 1) * P)
-                    back = psum.tile([P, HIDDEN], F32, tag="back")
-                    for t in range(PACK):
-                        nc.tensor.transpose(back[:, t * P : (t + 1) * P], hidden[:, t, cols], ident_f32[:])
-                    s2 = psum.tile([P, HIDDEN], F32, tag="s2")
-                    nc.tensor.matmul_mx(
-                        out=s2[:],
-                        lhsT=h_codes[:, cols].bitcast(FP8X4),
-                        lhsT_scale=h_scales[:, cols],
-                        rhs=w2_codes[:, g, :].bitcast(FP8X4),
-                        rhs_scale=w2_scales[:, g, :],
-                        start=True,
-                        stop=True,
-                    )
-                    pre = work.tile([P, HIDDEN], F32, bufs=4)
-                    nc.vector.tensor_tensor(out=pre[:], in0=s2[:], in1=b2_all[:, g, :], op=ADD)
-                    nc.vector.scalar_tensor_tensor(
-                        out=result[:, j, :], in0=pre[:], scalar=0.0, in1=back[:], op0=MAX, op1=ADD
-                    )
-                rows = slice(c * ROWS, (c + 1) * ROWS)
-                nc.sync.dma_start(out=out[rows, g, :].rearrange("(p j) n -> p j n", j=SUB), in_=result[:])
+        def layer2(u, j):
+            if not exists(u):
+                return
+            g = u % CODES
+            codes, scales = h_codes[u]
+            sums = psum.tile([P, HIDDEN], F32, tag="s2")
+            s2[(u, j)] = sums
+            nc.tensor.matmul_mx(
+                out=sums[:],
+                lhsT=codes[:, j * P : (j + 1) * P].bitcast(FP8X4),
+                lhsT_scale=scales[:, j * P : (j + 1) * P],
+                rhs=w2_codes[:, g, :].bitcast(FP8X4),
+                rhs_scale=w2_scales[:, g, :],
+                start=True,
+                stop=True,
+            )
+
+        def add_bias(u, j):
+            if not exists(u):
+                return
+            biased = work.tile([P, HIDDEN], F32, tag="pre", bufs=4)
+            pre[(u, j)] = biased
+            nc.vector.tensor_tensor(out=biased[:], in0=s2[(u, j)][:], in1=b2_all[:, u % CODES, :], op=ADD)
+
+        def finish(u, j):
+            if not exists(u):
+                return
+            c, g = divmod(u, CODES)
+            result = work.tile([P, HIDDEN], F32, tag="result", bufs=6)
+            nc.vector.scalar_tensor_tensor(
+                out=result[:], in0=pre[(u, j)][:], scalar=0.0, in1=back[(u, j)][:], op0=MAX, op1=ADD
+            )
+            rows = slice(c * ROWS, (c + 1) * ROWS)
+            nc.sync.dma_start(out=out[rows, g, :].rearrange("(p j) n -> p j n", j=SUB)[:, j, :], in_=result[:])
+
+        for u in range(2):
+            transpose_z(u, 0)
+            transpose_z(u, 1)
+        prepare_biases()
+        prepare_w1(0)
+        quantise_z(0)
+        prepare_w2(0, nc.scalar.copy)
+        prepare_w1(1)
+        quantise_z(1)
+        for t in range(PACK):
+            layer1(0, t)
+        prepare_w2(1, nc.vector.tensor_copy)
+        regroup_h(0)
+        quantise_h(0)
+        transpose_z(2, 0)
+        transpose_z(2, 1)
+        for t in range(PACK):
+            layer1(1, t)
+        quantise_z(2)
+        layer2(0, 0)
+        layer2(0, 1)
+
+        for i in range(UNITS):
+            regroup_h(i + 1)
+            residual_back(i, 0)
+            residual_back(i, 1)
+            add_bias(i, 0)
+            add_bias(i, 1)
+            layer1(i + 2, 0)
+            layer1(i + 2, 1)
+            layer2(i, 2)
+            layer2(i, 3)
+            finish(i, 0)
+            finish(i, 1)
+            quantise_h(i + 1)
+            residual_back(i, 2)
+            residual_back(i, 3)
+            transpose_z(i + 3, 0)
+            transpose_z(i + 3, 1)
+            add_bias(i, 2)
+            add_bias(i, 3)
+            layer1(i + 2, 2)
+            layer1(i + 2, 3)
+            layer2(i + 1, 0)
+            layer2(i + 1, 1)
+            finish(i, 2)
+            finish(i, 3)
+            quantise_z(i + 3)

@@ -10,6 +10,7 @@ U8 = mybir.dt.uint8
 FP8X4 = mybir.dt.float8_e4m3fn_x4
 ADD = mybir.AluOpType.add
 MAX = mybir.AluOpType.max
+MULT = mybir.AluOpType.mult
 RELU = mybir.ActivationFunctionType.Relu
 
 P = 128
@@ -22,7 +23,7 @@ ROWS = 512
 SUB = ROWS // P
 CHUNKS = BATCH // ROWS
 UNITS = CHUNKS * CODES
-SCALAR_SHARE = 3
+SCALAR_SHARE = 2
 
 FLOPS = 2 * BATCH * CODES * (2 * Z_HALF * HIDDEN + HIDDEN * HIDDEN)
 
@@ -189,13 +190,18 @@ def tile_linearwdecoder_pa_t_kernel(tc, z1, z2, W1, b1, W2, b2, out):
                 return
             grouped = work.tile([P, ROWS, PACK], BF16, tag="h_grouped", align_bytes=64)
             h_grouped[u] = grouped
-            for j in range(SUB):
+            for j in range(SCALAR_SHARE):
                 cols = slice(j * P, (j + 1) * P)
-                planes = hidden[u][:, :, cols].rearrange("p t b -> p b t")
-                if j < SCALAR_SHARE:
-                    nc.scalar.copy(out=grouped[:, cols, :], in_=planes)
-                else:
-                    nc.vector.tensor_copy(out=grouped[:, cols, :], in_=planes)
+                nc.scalar.copy(out=grouped[:, cols, :], in_=hidden[u][:, :, cols].rearrange("p t b -> p b t"))
+            rest = slice(SCALAR_SHARE * P, ROWS)
+            nc.gpsimd.tensor_scalar(
+                out=grouped[:, rest, :],
+                in0=hidden[u][:, :, rest].rearrange("p t b -> p b t"),
+                scalar1=1.0,
+                scalar2=0.0,
+                op0=MULT,
+                op1=ADD,
+            )
 
         def quantise_h(u):
             if not exists(u):

@@ -23,7 +23,7 @@ ROWS = 512
 SUB = ROWS // P
 CHUNKS = BATCH // ROWS
 UNITS = CHUNKS * CODES
-SCALAR_SHARE = 2
+SCALAR_SHARE = 1
 
 FLOPS = 2 * BATCH * CODES * (2 * Z_HALF * HIDDEN + HIDDEN * HIDDEN)
 
@@ -292,13 +292,13 @@ def tile_linearwdecoder_pa_t_kernel(tc, z1, z2, W1, b1, W2, b2, out):
             layer2(i, 3)
             finish(i, 0)
             finish(i, 1)
-            quantise_h(i + 1)
             residual_back(i, 2)
             residual_back(i, 3)
             transpose_z(i + 3, 0)
             transpose_z(i + 3, 1)
             add_bias(i, 2)
             add_bias(i, 3)
+            quantise_h(i + 1)
             layer1(i + 2, 2)
             layer1(i + 2, 3)
             layer2(i + 1, 0)

@@ -23,7 +23,8 @@ ROWS = 512
 SUB = ROWS // P
 CHUNKS = BATCH // ROWS
 UNITS = CHUNKS * CODES
-SCALAR_SHARE = 1
+PAIRS = 2
+SHIFTED = (0, 2)
 
 FLOPS = 2 * BATCH * CODES * (2 * Z_HALF * HIDDEN + HIDDEN * HIDDEN)
 
@@ -70,18 +71,21 @@ def tile_linearwdecoder_pa_t_kernel(tc, z1, z2, W1, b1, W2, b2, out):
         load_z(0)
         load_w(w1_raw, W1, 0)
         nc.sync.dma_start(out=bias_rows[0 : CODES * PACK, :], in_=b1.rearrange("g (a p) -> (g a) p", p=P))
-        load_w(w2_raw, W2, 0)
+        nc.sync.dma_start(out=bias_rows[CODES * PACK : 2 * CODES * PACK, :], in_=b2.rearrange("g (a p) -> (g a) p", p=P))
         load_w(w1_raw, W1, 1)
+        load_w(w2_raw, W2, 0)
+        load_z(1)
         load_w(w2_raw, W2, 1)
         nc.sync.dma_start(out=b2_bf16[:], in_=b2.rearrange("g n -> (g n)").partition_broadcast(P))
-        for c in range(1, CHUNKS):
+        for c in range(2, CHUNKS):
             load_z(c)
 
         w1_codes = const.tile([P, CODES, HIDDEN], U32, align_bytes=64)
         w1_scales = const.tile([P, CODES, HIDDEN], U8, align_bytes=64)
         w2_codes = const.tile([P, CODES, HIDDEN], U32, align_bytes=64)
         w2_scales = const.tile([P, CODES, HIDDEN], U8, align_bytes=64)
-        b1_col = const.tile([P, CODES * PACK], F32)
+        bias_col = const.tile([P, 2 * CODES * PACK], F32)
+        minus_b2_col = const.tile([P, CODES * PACK], F32)
         b2_all = const.tile([P, CODES, HIDDEN], F32)
 
         def words_onto_partitions(blocks, grouped_words, copy):
@@ -94,8 +98,8 @@ def tile_linearwdecoder_pa_t_kernel(tc, z1, z2, W1, b1, W2, b2, out):
         def prepare_biases():
             bias_flipped = psum.tile([P, P], BF16, tag="back")
             nc.tensor.transpose(bias_flipped[:], bias_rows[:], ident_bf16[:])
-            nc.vector.tensor_copy(out=b1_col[:], in_=bias_flipped[:, 0 : CODES * PACK])
-            nc.gpsimd.tensor_copy(out=b2_all[:].rearrange("p g n -> p (g n)"), in_=b2_bf16[:])
+            nc.vector.tensor_copy(out=bias_col[:], in_=bias_flipped[:, 0 : 2 * CODES * PACK])
+            nc.vector.tensor_scalar_mul(minus_b2_col[:], bias_col[:, CODES * PACK :], -1.0)
 
         def prepare_w1(g):
             w1_grouped = work.tile([P, HIDDEN * PACK], BF16, tag="w_grouped", align_bytes=64)
@@ -108,13 +112,15 @@ def tile_linearwdecoder_pa_t_kernel(tc, z1, z2, W1, b1, W2, b2, out):
                 words_onto_partitions(blocks, w1_words[:, h * 2 * P : (h + 1) * 2 * P, :], nc.vector.tensor_copy)
             nc.vector.quantize_mx(out=w1_codes[:, g, :].bitcast(FP8X4), scales=w1_scales[:, g, :], in_=w1_grouped[:])
 
-        def prepare_w2(g, copy):
+        def prepare_w2(g):
             w2_grouped = work.tile([P, HIDDEN, PACK], BF16, tag="w_grouped", align_bytes=64)
             for a in range(PACK):
                 w2_flipped = psum.tile([P, PACK, P], BF16, tag="back")
                 for t in range(PACK):
                     nc.tensor.transpose(w2_flipped[:, t, :], w2_raw[g][:, a, t * P : (t + 1) * P], ident_bf16[:])
-                copy(out=w2_grouped[:, a * P : (a + 1) * P, :], in_=w2_flipped[:].rearrange("k t c -> k c t"))
+                nc.vector.tensor_copy(
+                    out=w2_grouped[:, a * P : (a + 1) * P, :], in_=w2_flipped[:].rearrange("k t c -> k c t")
+                )
             nc.vector.quantize_mx(
                 out=w2_codes[:, g, :].bitcast(FP8X4),
                 scales=w2_scales[:, g, :],
@@ -126,12 +132,15 @@ def tile_linearwdecoder_pa_t_kernel(tc, z1, z2, W1, b1, W2, b2, out):
         hidden = {}
         h_grouped = {}
         h_codes = {}
+        summed = {}
         back = {}
-        s2 = {}
-        pre = {}
+        result = {}
 
         def exists(u):
             return 0 <= u < UNITS
+
+        def b2_block(u, t):
+            return CODES * PACK + (u % CODES) * PACK + t
 
         def transpose_z(u, h):
             if not exists(u):
@@ -181,7 +190,7 @@ def tile_linearwdecoder_pa_t_kernel(tc, z1, z2, W1, b1, W2, b2, out):
                 out=hidden[u][:, t, :],
                 in_=s1[:],
                 func=RELU,
-                bias=b1_col[:, g * PACK + t : g * PACK + t + 1],
+                bias=bias_col[:, g * PACK + t : g * PACK + t + 1],
                 scale=1.0,
             )
 
@@ -190,15 +199,25 @@ def tile_linearwdecoder_pa_t_kernel(tc, z1, z2, W1, b1, W2, b2, out):
                 return
             grouped = work.tile([P, ROWS, PACK], BF16, tag="h_grouped", align_bytes=64)
             h_grouped[u] = grouped
-            for j in range(SCALAR_SHARE):
+            for j in range(SUB):
                 cols = slice(j * P, (j + 1) * P)
-                nc.scalar.copy(out=grouped[:, cols, :], in_=hidden[u][:, :, cols].rearrange("p t b -> p b t"))
-            rest = slice(SCALAR_SHARE * P, ROWS)
+                nc.gpsimd.tensor_scalar(
+                    out=grouped[:, cols, :],
+                    in0=hidden[u][:, :, cols].rearrange("p t b -> p b t"),
+                    scalar1=1.0,
+                    scalar2=0.0,
+                    op0=MULT,
+                    op1=ADD,
+                )
+
+        def shift_residual(u, t):
+            if not exists(u):
+                return
             nc.gpsimd.tensor_scalar(
-                out=grouped[:, rest, :],
-                in0=hidden[u][:, :, rest].rearrange("p t b -> p b t"),
+                out=hidden[u][:, t, :],
+                in0=hidden[u][:, t, :],
                 scalar1=1.0,
-                scalar2=0.0,
+                scalar2=bias_col[:, b2_block(u, t) : b2_block(u, t) + 1],
                 op0=MULT,
                 op1=ADD,
             )
@@ -213,96 +232,100 @@ def tile_linearwdecoder_pa_t_kernel(tc, z1, z2, W1, b1, W2, b2, out):
                 out=codes[:].bitcast(FP8X4), scales=scales[:], in_=h_grouped[u][:].rearrange("p b t -> p (b t)")
             )
 
-        def residual_back(u, j):
-            if not exists(u):
-                return
-            rows_first = psum.tile([P, HIDDEN], F32, tag="back")
-            back[(u, j)] = rows_first
-            for t in range(PACK):
-                nc.tensor.transpose(
-                    rows_first[:, t * P : (t + 1) * P], hidden[u][:, t, j * P : (j + 1) * P], ident_f32[:]
-                )
-
-        def layer2(u, j):
+        def layer2(u, t):
             if not exists(u):
                 return
             g = u % CODES
             codes, scales = h_codes[u]
-            sums = psum.tile([P, HIDDEN], F32, tag="s2")
-            s2[(u, j)] = sums
+            s2 = psum.tile([P, ROWS], F32, tag="s2")
             nc.tensor.matmul_mx(
-                out=sums[:],
-                lhsT=codes[:, j * P : (j + 1) * P].bitcast(FP8X4),
-                lhsT_scale=scales[:, j * P : (j + 1) * P],
-                rhs=w2_codes[:, g, :].bitcast(FP8X4),
-                rhs_scale=w2_scales[:, g, :],
+                out=s2[:],
+                lhsT=w2_codes[:, g, t * P : (t + 1) * P].bitcast(FP8X4),
+                lhsT_scale=w2_scales[:, g, t * P : (t + 1) * P],
+                rhs=codes[:].bitcast(FP8X4),
+                rhs_scale=scales[:],
                 start=True,
                 stop=True,
             )
+            both = work.tile([P, ROWS], F32, tag="summed", bufs=4)
+            summed[(u, t)] = both
+            column = g * PACK + t
+            nc.vector.scalar_tensor_tensor(
+                out=both[:],
+                in0=s2[:],
+                scalar=minus_b2_col[:, column : column + 1],
+                in1=hidden[u][:, t, :],
+                op0=MAX,
+                op1=ADD,
+            )
 
-        def add_bias(u, j):
+        def rows_back(u, t):
             if not exists(u):
                 return
-            biased = work.tile([P, HIDDEN], F32, tag="pre", bufs=4)
-            pre[(u, j)] = biased
-            nc.vector.tensor_tensor(out=biased[:], in0=s2[(u, j)][:], in1=b2_all[:, u % CODES, :], op=ADD)
+            rows_first = psum.tile([P, SUB, P], F32, tag="back")
+            back[(u, t)] = rows_first
+            for j in range(SUB):
+                nc.tensor.transpose(rows_first[:, j, :], summed[(u, t)][:, j * P : (j + 1) * P], ident_f32[:])
 
-        def finish(u, j):
+        def finish(u, t):
+            if not exists(u):
+                return
+            if t == 0:
+                rows_out = work.tile([P, SUB, HIDDEN], F32, tag="result", bufs=3)
+                result[u] = rows_out
+            cols = slice(t * P, (t + 1) * P)
+            if t in SHIFTED:
+                nc.scalar.copy(out=result[u][:, :, cols], in_=back[(u, t)][:])
+            else:
+                nc.vector.tensor_tensor(
+                    out=result[u][:, :, cols],
+                    in0=back[(u, t)][:],
+                    in1=b2_all[:, u % CODES, cols].unsqueeze(1).to_broadcast([P, SUB, P]),
+                    op=ADD,
+                )
+
+        def store(u):
             if not exists(u):
                 return
             c, g = divmod(u, CODES)
-            result = work.tile([P, HIDDEN], F32, tag="result", bufs=6)
-            nc.vector.scalar_tensor_tensor(
-                out=result[:], in0=pre[(u, j)][:], scalar=0.0, in1=back[(u, j)][:], op0=MAX, op1=ADD
-            )
             rows = slice(c * ROWS, (c + 1) * ROWS)
-            nc.sync.dma_start(out=out[rows, g, :].rearrange("(p j) n -> p j n", j=SUB)[:, j, :], in_=result[:])
+            nc.sync.dma_start(out=out[rows, g, :].rearrange("(p j) n -> p j n", j=SUB), in_=result[u][:])
 
-        for u in range(2):
-            transpose_z(u, 0)
-            transpose_z(u, 1)
-        prepare_biases()
+        transpose_z(0, 0)
+        transpose_z(0, 1)
         prepare_w1(0)
+        prepare_biases()
         quantise_z(0)
-        prepare_w2(0, nc.scalar.copy)
+        transpose_z(1, 0)
+        transpose_z(1, 1)
         prepare_w1(1)
-        quantise_z(1)
-        for t in range(PACK):
-            layer1(0, t)
-        prepare_w2(1, nc.vector.tensor_copy)
-        regroup_h(0)
-        quantise_h(0)
-        transpose_z(2, 0)
-        transpose_z(2, 1)
-        for t in range(PACK):
-            layer1(1, t)
-        quantise_z(2)
-        layer2(0, 0)
-        layer2(0, 1)
 
-        for i in range(UNITS):
-            regroup_h(i + 1)
-            residual_back(i, 0)
-            residual_back(i, 1)
-            add_bias(i, 0)
-            add_bias(i, 1)
-            layer1(i + 2, 0)
-            layer1(i + 2, 1)
-            layer2(i, 2)
-            layer2(i, 3)
-            finish(i, 0)
-            finish(i, 1)
-            residual_back(i, 2)
-            residual_back(i, 3)
-            transpose_z(i + 3, 0)
-            transpose_z(i + 3, 1)
-            add_bias(i, 2)
-            add_bias(i, 3)
-            quantise_h(i + 1)
-            layer1(i + 2, 2)
-            layer1(i + 2, 3)
-            layer2(i + 1, 0)
-            layer2(i + 1, 1)
-            finish(i, 2)
-            finish(i, 3)
-            quantise_z(i + 3)
+        for k in range(PAIRS * UNITS + 6):
+            u, pair = divmod(k, PAIRS)
+            blocks = (PAIRS * pair, PAIRS * pair + 1)
+            if pair == 0:
+                quantise_z(u + 1)
+            else:
+                quantise_h(u - 1)
+            for t in blocks:
+                layer1(u, t)
+            for t in blocks:
+                layer2(u - 2, t)
+            transpose_z(u + 2, pair)
+            last_u, last_pair = divmod(k - 1, PAIRS)
+            last_blocks = (PAIRS * last_pair, PAIRS * last_pair + 1)
+            for t in last_blocks:
+                rows_back(last_u - 2, t)
+            for t in last_blocks:
+                finish(last_u - 2, t)
+            if last_pair == PAIRS - 1:
+                store(last_u - 2)
+            if pair == 1:
+                regroup_h(u)
+                for t in SHIFTED:
+                    shift_residual(u, t)
+            if k == 0:
+                prepare_w2(0)
+                nc.gpsimd.tensor_copy(out=b2_all[:].rearrange("p g n -> p (g n)"), in_=b2_bf16[:])
+            if k == 2:
+                prepare_w2(1)

@@ -12,6 +12,7 @@ ADD = mybir.AluOpType.add
 MAX = mybir.AluOpType.max
 MULT = mybir.AluOpType.mult
 RELU = mybir.ActivationFunctionType.Relu
+IDENTITY = mybir.ActivationFunctionType.Identity
 
 P = 128
 PACK = 4
@@ -24,7 +25,7 @@ SUB = ROWS // P
 CHUNKS = BATCH // ROWS
 UNITS = CHUNKS * CODES
 PAIRS = 2
-SHIFTED = (0, 2)
+SHIFTED = (1,)
 
 FLOPS = 2 * BATCH * CODES * (2 * Z_HALF * HIDDEN + HIDDEN * HIDDEN)
 
@@ -130,6 +131,7 @@ def tile_linearwdecoder_pa_t_kernel(tc, z1, z2, W1, b1, W2, b2, out):
         z_grouped = {}
         z_codes = {}
         hidden = {}
+        residual = {}
         h_grouped = {}
         h_codes = {}
         summed = {}
@@ -213,13 +215,14 @@ def tile_linearwdecoder_pa_t_kernel(tc, z1, z2, W1, b1, W2, b2, out):
         def shift_residual(u, t):
             if not exists(u):
                 return
-            nc.gpsimd.tensor_scalar(
-                out=hidden[u][:, t, :],
-                in0=hidden[u][:, t, :],
-                scalar1=1.0,
-                scalar2=bias_col[:, b2_block(u, t) : b2_block(u, t) + 1],
-                op0=MULT,
-                op1=ADD,
+            shifted = work.tile([P, ROWS], F32, tag="shifted", bufs=4)
+            residual[(u, t)] = shifted
+            nc.scalar.activation(
+                out=shifted[:],
+                in_=hidden[u][:, t, :],
+                func=IDENTITY,
+                bias=bias_col[:, b2_block(u, t) : b2_block(u, t) + 1],
+                scale=1.0,
             )
 
         def quantise_h(u):
@@ -247,6 +250,10 @@ def tile_linearwdecoder_pa_t_kernel(tc, z1, z2, W1, b1, W2, b2, out):
                 start=True,
                 stop=True,
             )
+            if t in SHIFTED:
+                carried = residual[(u, t)][:]
+            else:
+                carried = hidden[u][:, t, :]
             both = work.tile([P, ROWS], F32, tag="summed", bufs=4)
             summed[(u, t)] = both
             column = g * PACK + t
@@ -254,7 +261,7 @@ def tile_linearwdecoder_pa_t_kernel(tc, z1, z2, W1, b1, W2, b2, out):
                 out=both[:],
                 in0=s2[:],
                 scalar=minus_b2_col[:, column : column + 1],
-                in1=hidden[u][:, t, :],
+                in1=carried,
                 op0=MAX,
                 op1=ADD,
             )
@@ -312,6 +319,9 @@ def tile_linearwdecoder_pa_t_kernel(tc, z1, z2, W1, b1, W2, b2, out):
             for t in blocks:
                 layer2(u - 2, t)
             transpose_z(u + 2, pair)
+            for t in blocks:
+                if t in SHIFTED:
+                    shift_residual(u, t)
             last_u, last_pair = divmod(k - 1, PAIRS)
             last_blocks = (PAIRS * last_pair, PAIRS * last_pair + 1)
             for t in last_blocks:
@@ -322,8 +332,6 @@ def tile_linearwdecoder_pa_t_kernel(tc, z1, z2, W1, b1, W2, b2, out):
                 store(last_u - 2)
             if pair == 1:
                 regroup_h(u)
-                for t in SHIFTED:
-                    shift_residual(u, t)
             if k == 0:
                 prepare_w2(0)
                 nc.gpsimd.tensor_copy(out=b2_all[:].rearrange("p g n -> p (g n)"), in_=b2_bf16[:])

@@ -12,7 +12,6 @@ ADD = mybir.AluOpType.add
 MAX = mybir.AluOpType.max
 MULT = mybir.AluOpType.mult
 RELU = mybir.ActivationFunctionType.Relu
-IDENTITY = mybir.ActivationFunctionType.Identity
 
 P = 128
 PACK = 4
@@ -25,7 +24,10 @@ SUB = ROWS // P
 CHUNKS = BATCH // ROWS
 UNITS = CHUNKS * CODES
 PAIRS = 2
-SHIFTED = (1,)
+ON_TENSOR = (1,)
+
+SHARES = (("gpsimd", 0, 2), ("scalar", 2, 3), ("vector", 3, 4))
+FIRST = (("vector", 0, 2), ("gpsimd", 2, 3), ("scalar", 3, 4))
 
 FLOPS = 2 * BATCH * CODES * (2 * Z_HALF * HIDDEN + HIDDEN * HIDDEN)
 
@@ -62,6 +64,12 @@ def tile_linearwdecoder_pa_t_kernel(tc, z1, z2, W1, b1, W2, b2, out):
             nc.sync.dma_start(out=z_raw[c][0][:], in_=z1[rows, :].rearrange("(p j) k -> p j k", j=SUB))
             nc.sync.dma_start(out=z_raw[c][1][:], in_=z2[rows, :].rearrange("(p j) k -> p j k", j=SUB))
 
+        def load_z_code(c, g):
+            rows = slice(c * ROWS, (c + 1) * ROWS)
+            cols = slice(g * Z_HALF, (g + 1) * Z_HALF)
+            nc.sync.dma_start(out=z_raw[c][0][:, :, cols], in_=z1[rows, cols].rearrange("(p j) k -> p j k", j=SUB))
+            nc.sync.dma_start(out=z_raw[c][1][:, :, cols], in_=z2[rows, cols].rearrange("(p j) k -> p j k", j=SUB))
+
         def load_w(raw, w, g):
             nc.sync.dma_start(out=raw[g][:], in_=w[g].rearrange("(a p) k -> p a k", p=P))
 
@@ -69,10 +77,11 @@ def tile_linearwdecoder_pa_t_kernel(tc, z1, z2, W1, b1, W2, b2, out):
         nc.vector.memset(bias_rows[:], 0.0)
         b2_bf16 = const.tile([P, CODES * HIDDEN], BF16)
 
-        load_z(0)
         load_w(w1_raw, W1, 0)
+        load_z_code(0, 0)
         nc.sync.dma_start(out=bias_rows[0 : CODES * PACK, :], in_=b1.rearrange("g (a p) -> (g a) p", p=P))
         nc.sync.dma_start(out=bias_rows[CODES * PACK : 2 * CODES * PACK, :], in_=b2.rearrange("g (a p) -> (g a) p", p=P))
+        load_z_code(0, 1)
         load_w(w1_raw, W1, 1)
         load_w(w2_raw, W2, 0)
         load_z(1)
@@ -102,36 +111,43 @@ def tile_linearwdecoder_pa_t_kernel(tc, z1, z2, W1, b1, W2, b2, out):
             nc.vector.tensor_copy(out=bias_col[:], in_=bias_flipped[:, 0 : 2 * CODES * PACK])
             nc.vector.tensor_scalar_mul(minus_b2_col[:], bias_col[:, CODES * PACK :], -1.0)
 
-        def prepare_w1(g):
-            w1_grouped = work.tile([P, HIDDEN * PACK], BF16, tag="w_grouped", align_bytes=64)
-            w1_words = w1_grouped[:].bitcast(F32).rearrange("q (c u) -> q c u", u=2)
-            for h in range(2):
-                blocks = []
-                for a in (2 * h, 2 * h + 1):
-                    words = w1_raw[g][:, a, :].bitcast(F32)
-                    blocks.append((words[:, 0:P], words[:, P : 2 * P]))
-                words_onto_partitions(blocks, w1_words[:, h * 2 * P : (h + 1) * 2 * P, :], nc.vector.tensor_copy)
-            nc.vector.quantize_mx(out=w1_codes[:, g, :].bitcast(FP8X4), scales=w1_scales[:, g, :], in_=w1_grouped[:])
+        w_grouped = {}
 
-        def prepare_w2(g):
-            w2_grouped = work.tile([P, HIDDEN, PACK], BF16, tag="w_grouped", align_bytes=64)
-            for a in range(PACK):
-                w2_flipped = psum.tile([P, PACK, P], BF16, tag="back")
-                for t in range(PACK):
-                    nc.tensor.transpose(w2_flipped[:, t, :], w2_raw[g][:, a, t * P : (t + 1) * P], ident_bf16[:])
-                nc.vector.tensor_copy(
-                    out=w2_grouped[:, a * P : (a + 1) * P, :], in_=w2_flipped[:].rearrange("k t c -> k c t")
-                )
+        def flip_w1(g, h, copy):
+            if h == 0:
+                w1_grouped = work.tile([P, HIDDEN * PACK], BF16, tag="w_grouped", align_bytes=64)
+                w_grouped[(1, g)] = w1_grouped
+            w1_words = w_grouped[(1, g)][:].bitcast(F32).rearrange("q (c u) -> q c u", u=2)
+            blocks = []
+            for a in (2 * h, 2 * h + 1):
+                words = w1_raw[g][:, a, :].bitcast(F32)
+                blocks.append((words[:, 0:P], words[:, P : 2 * P]))
+            words_onto_partitions(blocks, w1_words[:, h * 2 * P : (h + 1) * 2 * P, :], copy)
+
+        def quantise_w1(g):
+            nc.vector.quantize_mx(
+                out=w1_codes[:, g, :].bitcast(FP8X4), scales=w1_scales[:, g, :], in_=w_grouped[(1, g)][:]
+            )
+
+        def flip_w2(g, a, copy):
+            if a == 0:
+                w2_grouped = work.tile([P, HIDDEN, PACK], BF16, tag="w_grouped", align_bytes=64)
+                w_grouped[(2, g)] = w2_grouped
+            w2_flipped = psum.tile([P, PACK, P], BF16, tag="back")
+            for t in range(PACK):
+                nc.tensor.transpose(w2_flipped[:, t, :], w2_raw[g][:, a, t * P : (t + 1) * P], ident_bf16[:])
+            copy(out=w_grouped[(2, g)][:, a * P : (a + 1) * P, :], in_=w2_flipped[:].rearrange("k t c -> k c t"))
+
+        def quantise_w2(g):
             nc.vector.quantize_mx(
                 out=w2_codes[:, g, :].bitcast(FP8X4),
                 scales=w2_scales[:, g, :],
-                in_=w2_grouped[:].rearrange("k c t -> k (c t)"),
+                in_=w_grouped[(2, g)][:].rearrange("k c t -> k (c t)"),
             )
 
         z_grouped = {}
         z_codes = {}
         hidden = {}
-        residual = {}
         h_grouped = {}
         h_codes = {}
         summed = {}
@@ -144,7 +160,7 @@ def tile_linearwdecoder_pa_t_kernel(tc, z1, z2, W1, b1, W2, b2, out):
         def b2_block(u, t):
             return CODES * PACK + (u % CODES) * PACK + t
 
-        def transpose_z(u, h):
+        def transpose_z(u, h, copy):
             if not exists(u):
                 return
             if h == 0:
@@ -160,7 +176,7 @@ def tile_linearwdecoder_pa_t_kernel(tc, z1, z2, W1, b1, W2, b2, out):
                         z_raw[c][1][:, j, :].bitcast(F32)[:, g * P : (g + 1) * P],
                     )
                 )
-            words_onto_partitions(blocks, z_words[:, h * 2 * P : (h + 1) * 2 * P, :], nc.scalar.copy)
+            words_onto_partitions(blocks, z_words[:, h * 2 * P : (h + 1) * 2 * P, :], copy)
 
         def quantise_z(u):
             if not exists(u):
@@ -196,34 +212,22 @@ def tile_linearwdecoder_pa_t_kernel(tc, z1, z2, W1, b1, W2, b2, out):
                 scale=1.0,
             )
 
-        def regroup_h(u):
+        def regroup_h(u, shares):
             if not exists(u):
                 return
             grouped = work.tile([P, ROWS, PACK], BF16, tag="h_grouped", align_bytes=64)
             h_grouped[u] = grouped
-            for j in range(SUB):
-                cols = slice(j * P, (j + 1) * P)
-                nc.gpsimd.tensor_scalar(
-                    out=grouped[:, cols, :],
-                    in0=hidden[u][:, :, cols].rearrange("p t b -> p b t"),
-                    scalar1=1.0,
-                    scalar2=0.0,
-                    op0=MULT,
-                    op1=ADD,
-                )
-
-        def shift_residual(u, t):
-            if not exists(u):
-                return
-            shifted = work.tile([P, ROWS], F32, tag="shifted", bufs=4)
-            residual[(u, t)] = shifted
-            nc.scalar.activation(
-                out=shifted[:],
-                in_=hidden[u][:, t, :],
-                func=IDENTITY,
-                bias=bias_col[:, b2_block(u, t) : b2_block(u, t) + 1],
-                scale=1.0,
-            )
+            for engine, first, last in shares:
+                cols = slice(first * P, last * P)
+                source = hidden[u][:, :, cols].rearrange("p t b -> p b t")
+                if engine == "gpsimd":
+                    nc.gpsimd.tensor_scalar(
+                        out=grouped[:, cols, :], in0=source, scalar1=1.0, scalar2=0.0, op0=MULT, op1=ADD
+                    )
+                elif engine == "scalar":
+                    nc.scalar.copy(out=grouped[:, cols, :], in_=source)
+                else:
+                    nc.vector.tensor_copy(out=grouped[:, cols, :], in_=source)
 
         def quantise_h(u):
             if not exists(u):
@@ -250,21 +254,26 @@ def tile_linearwdecoder_pa_t_kernel(tc, z1, z2, W1, b1, W2, b2, out):
                 start=True,
                 stop=True,
             )
-            if t in SHIFTED:
-                carried = residual[(u, t)][:]
-            else:
-                carried = hidden[u][:, t, :]
             both = work.tile([P, ROWS], F32, tag="summed", bufs=4)
             summed[(u, t)] = both
             column = g * PACK + t
-            nc.vector.scalar_tensor_tensor(
-                out=both[:],
-                in0=s2[:],
-                scalar=minus_b2_col[:, column : column + 1],
-                in1=carried,
-                op0=MAX,
-                op1=ADD,
-            )
+            if t in ON_TENSOR:
+                nc.scalar.activation(
+                    out=both[:],
+                    in_=s2[:],
+                    func=RELU,
+                    bias=bias_col[:, b2_block(u, t) : b2_block(u, t) + 1],
+                    scale=1.0,
+                )
+            else:
+                nc.vector.scalar_tensor_tensor(
+                    out=both[:],
+                    in0=s2[:],
+                    scalar=minus_b2_col[:, column : column + 1],
+                    in1=hidden[u][:, t, :],
+                    op0=MAX,
+                    op1=ADD,
+                )
 
         def rows_back(u, t):
             if not exists(u):
@@ -272,7 +281,20 @@ def tile_linearwdecoder_pa_t_kernel(tc, z1, z2, W1, b1, W2, b2, out):
             rows_first = psum.tile([P, SUB, P], F32, tag="back")
             back[(u, t)] = rows_first
             for j in range(SUB):
-                nc.tensor.transpose(rows_first[:, j, :], summed[(u, t)][:, j * P : (j + 1) * P], ident_f32[:])
+                rows = slice(j * P, (j + 1) * P)
+                if t in ON_TENSOR:
+                    addends = (hidden[u][:, t, rows], summed[(u, t)][:, rows])
+                else:
+                    addends = (summed[(u, t)][:, rows],)
+                for n, addend in enumerate(addends):
+                    nc.tensor.matmul(
+                        out=rows_first[:, j, :],
+                        lhsT=addend,
+                        rhs=ident_f32[:],
+                        start=(n == 0),
+                        stop=(n == len(addends) - 1),
+                        is_transpose=True,
+                    )
 
         def finish(u, t):
             if not exists(u):
@@ -281,7 +303,7 @@ def tile_linearwdecoder_pa_t_kernel(tc, z1, z2, W1, b1, W2, b2, out):
                 rows_out = work.tile([P, SUB, HIDDEN], F32, tag="result", bufs=3)
                 result[u] = rows_out
             cols = slice(t * P, (t + 1) * P)
-            if t in SHIFTED:
+            if t in ON_TENSOR:
                 nc.scalar.copy(out=result[u][:, :, cols], in_=back[(u, t)][:])
             else:
                 nc.vector.tensor_tensor(
@@ -291,49 +313,70 @@ def tile_linearwdecoder_pa_t_kernel(tc, z1, z2, W1, b1, W2, b2, out):
                     op=ADD,
                 )
 
-        def store(u):
+        def store(u, pair):
             if not exists(u):
                 return
             c, g = divmod(u, CODES)
             rows = slice(c * ROWS, (c + 1) * ROWS)
-            nc.sync.dma_start(out=out[rows, g, :].rearrange("(p j) n -> p j n", j=SUB), in_=result[u][:])
+            cols = slice(pair * 2 * P, (pair + 1) * 2 * P) if u == UNITS - 1 else slice(0, HIDDEN)
+            nc.sync.dma_start(
+                out=out[rows, g, cols].rearrange("(p j) n -> p j n", j=SUB), in_=result[u][:, :, cols]
+            )
 
-        transpose_z(0, 0)
-        transpose_z(0, 1)
-        prepare_w1(0)
-        prepare_biases()
+        flip_w1(0, 0, nc.vector.tensor_copy)
+        flip_w1(0, 1, nc.vector.tensor_copy)
+        transpose_z(0, 0, nc.scalar.copy)
+        transpose_z(0, 1, nc.vector.tensor_copy)
+        quantise_w1(0)
         quantise_z(0)
-        transpose_z(1, 0)
-        transpose_z(1, 1)
-        prepare_w1(1)
+        prepare_biases()
+        transpose_z(1, 0, nc.scalar.copy)
+        transpose_z(1, 1, nc.scalar.copy)
+        layer1(0, 0)
+        layer1(0, 1)
+        quantise_z(1)
+        flip_w1(1, 0, nc.vector.tensor_copy)
+        flip_w1(1, 1, nc.vector.tensor_copy)
+        quantise_w1(1)
+        layer1(0, 2)
+        layer1(0, 3)
+        for a in range(PACK):
+            flip_w2(0, a, nc.vector.tensor_copy)
+        regroup_h(0, FIRST)
+        quantise_w2(0)
+        layer1(1, 0)
+        layer1(1, 1)
+        quantise_h(0)
+        transpose_z(2, 0, nc.scalar.copy)
+        transpose_z(2, 1, nc.scalar.copy)
+        transpose_z(3, 0, nc.scalar.copy)
 
-        for k in range(PAIRS * UNITS + 6):
+        for k in range(3, PAIRS * UNITS + 5):
             u, pair = divmod(k, PAIRS)
             blocks = (PAIRS * pair, PAIRS * pair + 1)
-            if pair == 0:
+            u2, pair2 = divmod(k - 3, PAIRS)
+            blocks2 = (PAIRS * pair2, PAIRS * pair2 + 1)
+            u3, pair3 = divmod(k - 4, PAIRS)
+            blocks3 = (PAIRS * pair3, PAIRS * pair3 + 1)
+            if pair == 1:
                 quantise_z(u + 1)
-            else:
-                quantise_h(u - 1)
             for t in blocks:
                 layer1(u, t)
-            for t in blocks:
-                layer2(u - 2, t)
-            transpose_z(u + 2, pair)
-            for t in blocks:
-                if t in SHIFTED:
-                    shift_residual(u, t)
-            last_u, last_pair = divmod(k - 1, PAIRS)
-            last_blocks = (PAIRS * last_pair, PAIRS * last_pair + 1)
-            for t in last_blocks:
-                rows_back(last_u - 2, t)
-            for t in last_blocks:
-                finish(last_u - 2, t)
-            if last_pair == PAIRS - 1:
-                store(last_u - 2)
-            if pair == 1:
-                regroup_h(u)
-            if k == 0:
-                prepare_w2(0)
+            for t in blocks2:
+                layer2(u2, t)
+            transpose_z(u + 2, pair, nc.scalar.copy)
+            if pair == 0:
+                quantise_h(u - 1)
+            if k == 3:
+                for a in range(PACK):
+                    flip_w2(1, a, nc.vector.tensor_copy)
+                quantise_w2(1)
                 nc.gpsimd.tensor_copy(out=b2_all[:].rearrange("p g n -> p (g n)"), in_=b2_bf16[:])
-            if k == 2:
-                prepare_w2(1)
+            for t in blocks3:
+                rows_back(u3, t)
+            for t in blocks3:
+                finish(u3, t)
+            if pair3 == PAIRS - 1 or u3 == UNITS - 1:
+                store(u3, pair3)
+            if pair == 1:
+                regroup_h(u, FIRST if u == UNITS - 1 else SHARES)

@@ -29,6 +29,8 @@ ON_TENSOR = (1,)
 SHARES = (("gpsimd", 0, 2), ("scalar", 2, 3), ("vector", 3, 4))
 FIRST = (("vector", 0, 2), ("gpsimd", 2, 3), ("scalar", 3, 4))
 
+LAST_ON_TENSOR = (1, 3)
+
 FLOPS = 2 * BATCH * CODES * (2 * Z_HALF * HIDDEN + HIDDEN * HIDDEN)
 
 
@@ -99,14 +101,14 @@ def tile_linearwdecoder_pa_t_kernel(tc, z1, z2, W1, b1, W2, b2, out):
         b2_all = const.tile([P, CODES, HIDDEN], F32)
 
         def words_onto_partitions(blocks, grouped_words, copy):
-            flipped = psum.tile([P, 2, 2 * P], F32, tag="flipped")
+            flipped = psum.tile([P, 2, 2 * P], F32, tag="bank", bufs=8)
             for n, halves in enumerate(blocks):
                 for u, words in enumerate(halves):
                     nc.tensor.transpose(flipped[:, u, n * P : (n + 1) * P], words, ident_f32[:])
             copy(out=grouped_words, in_=flipped[:].rearrange("q u c -> q c u"))
 
         def prepare_biases():
-            bias_flipped = psum.tile([P, P], BF16, tag="back")
+            bias_flipped = psum.tile([P, P], BF16, tag="bank", bufs=8)
             nc.tensor.transpose(bias_flipped[:], bias_rows[:], ident_bf16[:])
             nc.vector.tensor_copy(out=bias_col[:], in_=bias_flipped[:, 0 : 2 * CODES * PACK])
             nc.vector.tensor_scalar_mul(minus_b2_col[:], bias_col[:, CODES * PACK :], -1.0)
@@ -133,7 +135,7 @@ def tile_linearwdecoder_pa_t_kernel(tc, z1, z2, W1, b1, W2, b2, out):
             if a == 0:
                 w2_grouped = work.tile([P, HIDDEN, PACK], BF16, tag="w_grouped", align_bytes=64)
                 w_grouped[(2, g)] = w2_grouped
-            w2_flipped = psum.tile([P, PACK, P], BF16, tag="back")
+            w2_flipped = psum.tile([P, PACK, P], BF16, tag="bank", bufs=8)
             for t in range(PACK):
                 nc.tensor.transpose(w2_flipped[:, t, :], w2_raw[g][:, a, t * P : (t + 1) * P], ident_bf16[:])
             copy(out=w_grouped[(2, g)][:, a * P : (a + 1) * P, :], in_=w2_flipped[:].rearrange("k t c -> k c t"))
@@ -156,6 +158,9 @@ def tile_linearwdecoder_pa_t_kernel(tc, z1, z2, W1, b1, W2, b2, out):
 
         def exists(u):
             return 0 <= u < UNITS
+
+        def on_tensor(u, t):
+            return t in (LAST_ON_TENSOR if u >= UNITS - 2 else ON_TENSOR)
 
         def b2_block(u, t):
             return CODES * PACK + (u % CODES) * PACK + t
@@ -194,7 +199,7 @@ def tile_linearwdecoder_pa_t_kernel(tc, z1, z2, W1, b1, W2, b2, out):
                 hidden[u] = planes
             g = u % CODES
             codes, scales = z_codes[u]
-            s1 = psum.tile([P, ROWS], F32, tag="s1")
+            s1 = psum.tile([P, ROWS], F32, tag="bank", bufs=8)
             nc.tensor.matmul_mx(
                 out=s1[:],
                 lhsT=w1_codes[:, g, t * P : (t + 1) * P].bitcast(FP8X4),
@@ -244,7 +249,7 @@ def tile_linearwdecoder_pa_t_kernel(tc, z1, z2, W1, b1, W2, b2, out):
                 return
             g = u % CODES
             codes, scales = h_codes[u]
-            s2 = psum.tile([P, ROWS], F32, tag="s2")
+            s2 = psum.tile([P, ROWS], F32, tag="bank", bufs=8)
             nc.tensor.matmul_mx(
                 out=s2[:],
                 lhsT=w2_codes[:, g, t * P : (t + 1) * P].bitcast(FP8X4),
@@ -257,7 +262,7 @@ def tile_linearwdecoder_pa_t_kernel(tc, z1, z2, W1, b1, W2, b2, out):
             both = work.tile([P, ROWS], F32, tag="summed", bufs=4)
             summed[(u, t)] = both
             column = g * PACK + t
-            if t in ON_TENSOR:
+            if on_tensor(u, t):
                 nc.scalar.activation(
                     out=both[:],
                     in_=s2[:],
@@ -278,11 +283,11 @@ def tile_linearwdecoder_pa_t_kernel(tc, z1, z2, W1, b1, W2, b2, out):
         def rows_back(u, t):
             if not exists(u):
                 return
-            rows_first = psum.tile([P, SUB, P], F32, tag="back")
+            rows_first = psum.tile([P, SUB, P], F32, tag="bank", bufs=8)
             back[(u, t)] = rows_first
             for j in range(SUB):
                 rows = slice(j * P, (j + 1) * P)
-                if t in ON_TENSOR:
+                if on_tensor(u, t):
                     addends = (hidden[u][:, t, rows], summed[(u, t)][:, rows])
                 else:
                     addends = (summed[(u, t)][:, rows],)
@@ -303,7 +308,7 @@ def tile_linearwdecoder_pa_t_kernel(tc, z1, z2, W1, b1, W2, b2, out):
                 rows_out = work.tile([P, SUB, HIDDEN], F32, tag="result", bufs=3)
                 result[u] = rows_out
             cols = slice(t * P, (t + 1) * P)
-            if t in ON_TENSOR:
+            if on_tensor(u, t):
                 nc.scalar.copy(out=result[u][:, :, cols], in_=back[(u, t)][:])
             else:
                 nc.vector.tensor_tensor(
@@ -318,7 +323,7 @@ def tile_linearwdecoder_pa_t_kernel(tc, z1, z2, W1, b1, W2, b2, out):
                 return
             c, g = divmod(u, CODES)
             rows = slice(c * ROWS, (c + 1) * ROWS)
-            cols = slice(pair * 2 * P, (pair + 1) * 2 * P) if u == UNITS - 1 else slice(0, HIDDEN)
+            cols = slice(pair * P, (pair + 1) * P) if u == UNITS - 1 else slice(0, HIDDEN)
             nc.sync.dma_start(
                 out=out[rows, g, cols].rearrange("(p j) n -> p j n", j=SUB), in_=result[u][:, :, cols]
             )
@@ -326,7 +331,7 @@ def tile_linearwdecoder_pa_t_kernel(tc, z1, z2, W1, b1, W2, b2, out):
         flip_w1(0, 0, nc.vector.tensor_copy)
         flip_w1(0, 1, nc.vector.tensor_copy)
         transpose_z(0, 0, nc.scalar.copy)
-        transpose_z(0, 1, nc.vector.tensor_copy)
+        transpose_z(0, 1, nc.scalar.copy)
         quantise_w1(0)
         quantise_z(0)
         prepare_biases()
@@ -376,7 +381,7 @@ def tile_linearwdecoder_pa_t_kernel(tc, z1, z2, W1, b1, W2, b2, out):
                 rows_back(u3, t)
             for t in blocks3:
                 finish(u3, t)
-            if pair3 == PAIRS - 1 or u3 == UNITS - 1:
-                store(u3, pair3)
+                if t == PACK - 1 or u3 == UNITS - 1:
+                    store(u3, t)
             if pair == 1:
                 regroup_h(u, FIRST if u == UNITS - 1 else SHARES)

@@ -24,9 +24,9 @@ SUB = ROWS // P
 CHUNKS = BATCH // ROWS
 UNITS = CHUNKS * CODES
 PAIRS = 2
-ON_TENSOR = (1,)
+ON_TENSOR = (3,)
 
-SHARES = (("gpsimd", 0, 2), ("scalar", 2, 3), ("vector", 3, 4))
+SHARES = (("gpsimd", 0, 1), ("gpsimd", 1, 2), ("gpsimd", 2, 3), ("gpsimd", 3, 4))
 FIRST = (("vector", 0, 2), ("gpsimd", 2, 3), ("scalar", 3, 4))
 
 LAST_ON_TENSOR = (1, 3)
@@ -354,34 +354,33 @@ def tile_linearwdecoder_pa_t_kernel(tc, z1, z2, W1, b1, W2, b2, out):
         quantise_h(0)
         transpose_z(2, 0, nc.scalar.copy)
         transpose_z(2, 1, nc.scalar.copy)
+        layer1(1, 2)
+        layer1(1, 3)
+        quantise_z(2)
+        for a in range(PACK):
+            flip_w2(1, a, nc.vector.tensor_copy)
+        quantise_w2(1)
+        nc.gpsimd.tensor_copy(out=b2_all[:].rearrange("p g n -> p (g n)"), in_=b2_bf16[:])
         transpose_z(3, 0, nc.scalar.copy)
+        transpose_z(3, 1, nc.scalar.copy)
+        regroup_h(1, FIRST)
 
-        for k in range(3, PAIRS * UNITS + 5):
-            u, pair = divmod(k, PAIRS)
-            blocks = (PAIRS * pair, PAIRS * pair + 1)
-            u2, pair2 = divmod(k - 3, PAIRS)
-            blocks2 = (PAIRS * pair2, PAIRS * pair2 + 1)
-            u3, pair3 = divmod(k - 4, PAIRS)
-            blocks3 = (PAIRS * pair3, PAIRS * pair3 + 1)
-            if pair == 1:
-                quantise_z(u + 1)
-            for t in blocks:
-                layer1(u, t)
-            for t in blocks2:
-                layer2(u2, t)
-            transpose_z(u + 2, pair, nc.scalar.copy)
-            if pair == 0:
-                quantise_h(u - 1)
-            if k == 3:
-                for a in range(PACK):
-                    flip_w2(1, a, nc.vector.tensor_copy)
-                quantise_w2(1)
-                nc.gpsimd.tensor_copy(out=b2_all[:].rearrange("p g n -> p (g n)"), in_=b2_bf16[:])
-            for t in blocks3:
-                rows_back(u3, t)
-            for t in blocks3:
-                finish(u3, t)
-                if t == PACK - 1 or u3 == UNITS - 1:
-                    store(u3, t)
-            if pair == 1:
-                regroup_h(u, FIRST if u == UNITS - 1 else SHARES)
+        for u in range(2, UNITS + 2):
+            layer1(u, 0)
+            layer2(u - 2, 0)
+            layer1(u, 1)
+            layer2(u - 2, 1)
+            layer1(u, 2)
+            layer2(u - 2, 2)
+            layer1(u, 3)
+            layer2(u - 2, 3)
+            transpose_z(u + 2, 0, nc.scalar.copy)
+            transpose_z(u + 2, 1, nc.scalar.copy)
+            quantise_z(u + 1)
+            quantise_h(u - 1)
+            for t in range(PACK):
+                rows_back(u - 2, t)
+                finish(u - 2, t)
+                if t == PACK - 1 or u - 2 == UNITS - 1:
+                    store(u - 2, t)
+            regroup_h(u, FIRST if u == UNITS - 1 else SHARES)

@@ -29,8 +29,6 @@ ON_TENSOR = (3,)
 SHARES = (("gpsimd", 0, 1), ("gpsimd", 1, 2), ("gpsimd", 2, 3), ("gpsimd", 3, 4))
 FIRST = (("vector", 0, 2), ("gpsimd", 2, 3), ("scalar", 3, 4))
 
-LAST_ON_TENSOR = (1, 3)
-
 FLOPS = 2 * BATCH * CODES * (2 * Z_HALF * HIDDEN + HIDDEN * HIDDEN)
 
 
@@ -159,9 +157,6 @@ def tile_linearwdecoder_pa_t_kernel(tc, z1, z2, W1, b1, W2, b2, out):
         def exists(u):
             return 0 <= u < UNITS
 
-        def on_tensor(u, t):
-            return t in (LAST_ON_TENSOR if u >= UNITS - 2 else ON_TENSOR)
-
         def b2_block(u, t):
             return CODES * PACK + (u % CODES) * PACK + t
 
@@ -262,7 +257,7 @@ def tile_linearwdecoder_pa_t_kernel(tc, z1, z2, W1, b1, W2, b2, out):
             both = work.tile([P, ROWS], F32, tag="summed", bufs=4)
             summed[(u, t)] = both
             column = g * PACK + t
-            if on_tensor(u, t):
+            if t in ON_TENSOR:
                 nc.scalar.activation(
                     out=both[:],
                     in_=s2[:],
@@ -287,7 +282,7 @@ def tile_linearwdecoder_pa_t_kernel(tc, z1, z2, W1, b1, W2, b2, out):
             back[(u, t)] = rows_first
             for j in range(SUB):
                 rows = slice(j * P, (j + 1) * P)
-                if on_tensor(u, t):
+                if t in ON_TENSOR:
                     addends = (hidden[u][:, t, rows], summed[(u, t)][:, rows])
                 else:
                     addends = (summed[(u, t)][:, rows],)
@@ -308,7 +303,7 @@ def tile_linearwdecoder_pa_t_kernel(tc, z1, z2, W1, b1, W2, b2, out):
                 rows_out = work.tile([P, SUB, HIDDEN], F32, tag="result", bufs=3)
                 result[u] = rows_out
             cols = slice(t * P, (t + 1) * P)
-            if on_tensor(u, t):
+            if t in ON_TENSOR:
                 nc.scalar.copy(out=result[u][:, :, cols], in_=back[(u, t)][:])
             else:
                 nc.vector.tensor_tensor(
@@ -363,7 +358,7 @@ def tile_linearwdecoder_pa_t_kernel(tc, z1, z2, W1, b1, W2, b2, out):
         nc.gpsimd.tensor_copy(out=b2_all[:].rearrange("p g n -> p (g n)"), in_=b2_bf16[:])
         transpose_z(3, 0, nc.scalar.copy)
         transpose_z(3, 1, nc.scalar.copy)
-        regroup_h(1, FIRST)
+        regroup_h(1, SHARES)
 
         for u in range(2, UNITS + 2):
             layer1(u, 0)
@@ -383,4 +378,4 @@ def tile_linearwdecoder_pa_t_kernel(tc, z1, z2, W1, b1, W2, b2, out):
                 finish(u - 2, t)
                 if t == PACK - 1 or u - 2 == UNITS - 1:
                     store(u - 2, t)
-            regroup_h(u, FIRST if u == UNITS - 1 else SHARES)
+            regroup_h(u, SHARES)

from contextlib import ExitStack

import concourse.mybir as mybir
from concourse.masks import make_identity

F32 = mybir.dt.float32
BF16 = mybir.dt.bfloat16
U32 = mybir.dt.uint32
U8 = mybir.dt.uint8
FP8X4 = mybir.dt.float8_e4m3fn_x4
ADD = mybir.AluOpType.add
MAX = mybir.AluOpType.max
MULT = mybir.AluOpType.mult
RELU = mybir.ActivationFunctionType.Relu

P = 128
PACK = 4
BATCH = 4096
CODES = 2
Z_HALF = 256
HIDDEN = 512
ROWS = 512
SUB = ROWS // P
CHUNKS = BATCH // ROWS
UNITS = CHUNKS * CODES
PAIRS = 2
ON_TENSOR = (3,)

SHARES = (("gpsimd", 0, 1), ("gpsimd", 1, 2), ("gpsimd", 2, 3), ("gpsimd", 3, 4))
FIRST = (("vector", 0, 2), ("gpsimd", 2, 3), ("scalar", 3, 4))

FLOPS = 2 * BATCH * CODES * (2 * Z_HALF * HIDDEN + HIDDEN * HIDDEN)


def tile_linearwdecoder_pa_t_kernel(tc, z1, z2, W1, b1, W2, b2, out):
    nc = tc.nc
    with ExitStack() as ctx:
        const = ctx.enter_context(tc.tile_pool(name="const", bufs=1))
        inputs = ctx.enter_context(tc.tile_pool(name="inputs", bufs=1))
        work = ctx.enter_context(tc.tile_pool(name="work", bufs=2))
        psum = ctx.enter_context(tc.psum_pool(name="psum", bufs=2))
        ctx.enter_context(tc.manual_schedule())

        ident_f32 = const.tile([P, P], F32)
        make_identity(nc, ident_f32[:])
        ident_bf16 = const.tile([P, P], BF16)
        make_identity(nc, ident_bf16[:])

        w1_raw = []
        w2_raw = []
        z_raw = []
        for g in range(CODES):
            w1_g = inputs.tile([P, PACK, HIDDEN], BF16, name="w1_raw_%d" % g)
            w1_raw.append(w1_g)
            w2_g = inputs.tile([P, PACK, HIDDEN], BF16, name="w2_raw_%d" % g)
            w2_raw.append(w2_g)
        for c in range(CHUNKS):
            z1_c = inputs.tile([P, SUB, CODES * Z_HALF], BF16, name="z1_raw_%d" % c)
            z2_c = inputs.tile([P, SUB, CODES * Z_HALF], BF16, name="z2_raw_%d" % c)
            z_raw.append((z1_c, z2_c))

        def load_z(c):
            rows = slice(c * ROWS, (c + 1) * ROWS)
            nc.sync.dma_start(out=z_raw[c][0][:], in_=z1[rows, :].rearrange("(p j) k -> p j k", j=SUB))
            nc.sync.dma_start(out=z_raw[c][1][:], in_=z2[rows, :].rearrange("(p j) k -> p j k", j=SUB))

        def load_z_code(c, g):
            rows = slice(c * ROWS, (c + 1) * ROWS)
            cols = slice(g * Z_HALF, (g + 1) * Z_HALF)
            nc.sync.dma_start(out=z_raw[c][0][:, :, cols], in_=z1[rows, cols].rearrange("(p j) k -> p j k", j=SUB))
            nc.sync.dma_start(out=z_raw[c][1][:, :, cols], in_=z2[rows, cols].rearrange("(p j) k -> p j k", j=SUB))

        def load_w(raw, w, g):
            nc.sync.dma_start(out=raw[g][:], in_=w[g].rearrange("(a p) k -> p a k", p=P))

        bias_rows = const.tile([P, P], BF16)
        nc.vector.memset(bias_rows[:], 0.0)
        b2_bf16 = const.tile([P, CODES * HIDDEN], BF16)

        load_w(w1_raw, W1, 0)
        load_z_code(0, 0)
        nc.sync.dma_start(out=bias_rows[0 : CODES * PACK, :], in_=b1.rearrange("g (a p) -> (g a) p", p=P))
        nc.sync.dma_start(out=bias_rows[CODES * PACK : 2 * CODES * PACK, :], in_=b2.rearrange("g (a p) -> (g a) p", p=P))
        load_z_code(0, 1)
        load_w(w1_raw, W1, 1)
        load_w(w2_raw, W2, 0)
        load_z(1)
        load_w(w2_raw, W2, 1)
        nc.sync.dma_start(out=b2_bf16[:], in_=b2.rearrange("g n -> (g n)").partition_broadcast(P))
        for c in range(2, CHUNKS):
            load_z(c)

        w1_codes = const.tile([P, CODES, HIDDEN], U32, align_bytes=64)
        w1_scales = const.tile([P, CODES, HIDDEN], U8, align_bytes=64)
        w2_codes = const.tile([P, CODES, HIDDEN], U32, align_bytes=64)
        w2_scales = const.tile([P, CODES, HIDDEN], U8, align_bytes=64)
        bias_col = const.tile([P, 2 * CODES * PACK], F32)
        minus_b2_col = const.tile([P, CODES * PACK], F32)
        b2_all = const.tile([P, CODES, HIDDEN], F32)

        def words_onto_partitions(blocks, grouped_words, copy):
            flipped = psum.tile([P, 2, 2 * P], F32, tag="bank", bufs=8)
            for n, halves in enumerate(blocks):
                for u, words in enumerate(halves):
                    nc.tensor.transpose(flipped[:, u, n * P : (n + 1) * P], words, ident_f32[:])
            copy(out=grouped_words, in_=flipped[:].rearrange("q u c -> q c u"))

        def prepare_biases():
            bias_flipped = psum.tile([P, P], BF16, tag="bank", bufs=8)
            nc.tensor.transpose(bias_flipped[:], bias_rows[:], ident_bf16[:])
            nc.vector.tensor_copy(out=bias_col[:], in_=bias_flipped[:, 0 : 2 * CODES * PACK])
            nc.vector.tensor_scalar_mul(minus_b2_col[:], bias_col[:, CODES * PACK :], -1.0)

        w_grouped = {}

        def flip_w1(g, h, copy):
            if h == 0:
                w1_grouped = work.tile([P, HIDDEN * PACK], BF16, tag="w_grouped", align_bytes=64)
                w_grouped[(1, g)] = w1_grouped
            w1_words = w_grouped[(1, g)][:].bitcast(F32).rearrange("q (c u) -> q c u", u=2)
            blocks = []
            for a in (2 * h, 2 * h + 1):
                words = w1_raw[g][:, a, :].bitcast(F32)
                blocks.append((words[:, 0:P], words[:, P : 2 * P]))
            words_onto_partitions(blocks, w1_words[:, h * 2 * P : (h + 1) * 2 * P, :], copy)

        def quantise_w1(g):
            nc.vector.quantize_mx(
                out=w1_codes[:, g, :].bitcast(FP8X4), scales=w1_scales[:, g, :], in_=w_grouped[(1, g)][:]
            )

        def flip_w2(g, a, copy):
            if a == 0:
                w2_grouped = work.tile([P, HIDDEN, PACK], BF16, tag="w_grouped", align_bytes=64)
                w_grouped[(2, g)] = w2_grouped
            w2_flipped = psum.tile([P, PACK, P], BF16, tag="bank", bufs=8)
            for t in range(PACK):
                nc.tensor.transpose(w2_flipped[:, t, :], w2_raw[g][:, a, t * P : (t + 1) * P], ident_bf16[:])
            copy(out=w_grouped[(2, g)][:, a * P : (a + 1) * P, :], in_=w2_flipped[:].rearrange("k t c -> k c t"))

        def quantise_w2(g):
            nc.vector.quantize_mx(
                out=w2_codes[:, g, :].bitcast(FP8X4),
                scales=w2_scales[:, g, :],
                in_=w_grouped[(2, g)][:].rearrange("k c t -> k (c t)"),
            )

        z_grouped = {}
        z_codes = {}
        hidden = {}
        h_grouped = {}
        h_codes = {}
        summed = {}
        back = {}
        result = {}

        def exists(u):
            return 0 <= u < UNITS

        def b2_block(u, t):
            return CODES * PACK + (u % CODES) * PACK + t

        def transpose_z(u, h, copy):
            if not exists(u):
                return
            if h == 0:
                grouped = work.tile([P, ROWS * PACK], BF16, tag="z_grouped", bufs=3, align_bytes=64)
                z_grouped[u] = grouped
            c, g = divmod(u, CODES)
            z_words = z_grouped[u][:].bitcast(F32).rearrange("q (c u) -> q c u", u=2)
            blocks = []
            for j in (2 * h, 2 * h + 1):
                blocks.append(
                    (
                        z_raw[c][0][:, j, :].bitcast(F32)[:, g * P : (g + 1) * P],
                        z_raw[c][1][:, j, :].bitcast(F32)[:, g * P : (g + 1) * P],
                    )
                )
            words_onto_partitions(blocks, z_words[:, h * 2 * P : (h + 1) * 2 * P, :], copy)

        def quantise_z(u):
            if not exists(u):
                return
            codes = work.tile([P, ROWS], U32, tag="z_codes", align_bytes=64)
            scales = work.tile([P, ROWS], U8, tag="z_scales", align_bytes=64)
            z_codes[u] = (codes, scales)
            nc.vector.quantize_mx(out=codes[:].bitcast(FP8X4), scales=scales[:], in_=z_grouped[u][:])

        def layer1(u, t):
            if not exists(u):
                return
            if t == 0:
                planes = work.tile([P, PACK, ROWS], F32, tag="hidden", bufs=4)
                hidden[u] = planes
            g = u % CODES
            codes, scales = z_codes[u]
            s1 = psum.tile([P, ROWS], F32, tag="bank", bufs=8)
            nc.tensor.matmul_mx(
                out=s1[:],
                lhsT=w1_codes[:, g, t * P : (t + 1) * P].bitcast(FP8X4),
                lhsT_scale=w1_scales[:, g, t * P : (t + 1) * P],
                rhs=codes[:].bitcast(FP8X4),
                rhs_scale=scales[:],
                start=True,
                stop=True,
            )
            nc.scalar.activation(
                out=hidden[u][:, t, :],
                in_=s1[:],
                func=RELU,
                bias=bias_col[:, g * PACK + t : g * PACK + t + 1],
                scale=1.0,
            )

        def regroup_h(u, shares):
            if not exists(u):
                return
            grouped = work.tile([P, ROWS, PACK], BF16, tag="h_grouped", align_bytes=64)
            h_grouped[u] = grouped
            for engine, first, last in shares:
                cols = slice(first * P, last * P)
                source = hidden[u][:, :, cols].rearrange("p t b -> p b t")
                if engine == "gpsimd":
                    nc.gpsimd.tensor_scalar(
                        out=grouped[:, cols, :], in0=source, scalar1=1.0, scalar2=0.0, op0=MULT, op1=ADD
                    )
                elif engine == "scalar":
                    nc.scalar.copy(out=grouped[:, cols, :], in_=source)
                else:
                    nc.vector.tensor_copy(out=grouped[:, cols, :], in_=source)

        def quantise_h(u):
            if not exists(u):
                return
            codes = work.tile([P, ROWS], U32, tag="h_codes", align_bytes=64)
            scales = work.tile([P, ROWS], U8, tag="h_scales", align_bytes=64)
            h_codes[u] = (codes, scales)
            nc.vector.quantize_mx(
                out=codes[:].bitcast(FP8X4), scales=scales[:], in_=h_grouped[u][:].rearrange("p b t -> p (b t)")
            )

        def layer2(u, t):
            if not exists(u):
                return
            g = u % CODES
            codes, scales = h_codes[u]
            s2 = psum.tile([P, ROWS], F32, tag="bank", bufs=8)
            nc.tensor.matmul_mx(
                out=s2[:],
                lhsT=w2_codes[:, g, t * P : (t + 1) * P].bitcast(FP8X4),
                lhsT_scale=w2_scales[:, g, t * P : (t + 1) * P],
                rhs=codes[:].bitcast(FP8X4),
                rhs_scale=scales[:],
                start=True,
                stop=True,
            )
            both = work.tile([P, ROWS], F32, tag="summed", bufs=4)
            summed[(u, t)] = both
            column = g * PACK + t
            if t in ON_TENSOR:
                nc.scalar.activation(
                    out=both[:],
                    in_=s2[:],
                    func=RELU,
                    bias=bias_col[:, b2_block(u, t) : b2_block(u, t) + 1],
                    scale=1.0,
                )
            else:
                nc.vector.scalar_tensor_tensor(
                    out=both[:],
                    in0=s2[:],
                    scalar=minus_b2_col[:, column : column + 1],
                    in1=hidden[u][:, t, :],
                    op0=MAX,
                    op1=ADD,
                )

        def rows_back(u, t):
            if not exists(u):
                return
            rows_first = psum.tile([P, SUB, P], F32, tag="bank", bufs=8)
            back[(u, t)] = rows_first
            for j in range(SUB):
                rows = slice(j * P, (j + 1) * P)
                if t in ON_TENSOR:
                    addends = (hidden[u][:, t, rows], summed[(u, t)][:, rows])
                else:
                    addends = (summed[(u, t)][:, rows],)
                for n, addend in enumerate(addends):
                    nc.tensor.matmul(
                        out=rows_first[:, j, :],
                        lhsT=addend,
                        rhs=ident_f32[:],
                        start=(n == 0),
                        stop=(n == len(addends) - 1),
                        is_transpose=True,
                    )

        def finish(u, t):
            if not exists(u):
                return
            if t == 0:
                rows_out = work.tile([P, SUB, HIDDEN], F32, tag="result", bufs=3)
                result[u] = rows_out
            cols = slice(t * P, (t + 1) * P)
            if t in ON_TENSOR:
                nc.scalar.copy(out=result[u][:, :, cols], in_=back[(u, t)][:])
            else:
                nc.vector.tensor_tensor(
                    out=result[u][:, :, cols],
                    in0=back[(u, t)][:],
                    in1=b2_all[:, u % CODES, cols].unsqueeze(1).to_broadcast([P, SUB, P]),
                    op=ADD,
                )

        def store(u, pair):
            if not exists(u):
                return
            c, g = divmod(u, CODES)
            rows = slice(c * ROWS, (c + 1) * ROWS)
            cols = slice(pair * P, (pair + 1) * P) if u == UNITS - 1 else slice(0, HIDDEN)
            nc.sync.dma_start(
                out=out[rows, g, cols].rearrange("(p j) n -> p j n", j=SUB), in_=result[u][:, :, cols]
            )

        flip_w1(0, 0, nc.vector.tensor_copy)
        flip_w1(0, 1, nc.vector.tensor_copy)
        transpose_z(0, 0, nc.scalar.copy)
        transpose_z(0, 1, nc.scalar.copy)
        quantise_w1(0)
        quantise_z(0)
        prepare_biases()
        transpose_z(1, 0, nc.scalar.copy)
        transpose_z(1, 1, nc.scalar.copy)
        layer1(0, 0)
        layer1(0, 1)
        quantise_z(1)
        flip_w1(1, 0, nc.vector.tensor_copy)
        flip_w1(1, 1, nc.vector.tensor_copy)
        quantise_w1(1)
        layer1(0, 2)
        layer1(0, 3)
        for a in range(PACK):
            flip_w2(0, a, nc.vector.tensor_copy)
        regroup_h(0, FIRST)
        quantise_w2(0)
        layer1(1, 0)
        layer1(1, 1)
        quantise_h(0)
        transpose_z(2, 0, nc.scalar.copy)
        transpose_z(2, 1, nc.scalar.copy)
        layer1(1, 2)
        layer1(1, 3)
        quantise_z(2)
        for a in range(PACK):
            flip_w2(1, a, nc.vector.tensor_copy)
        quantise_w2(1)
        nc.gpsimd.tensor_copy(out=b2_all[:].rearrange("p g n -> p (g n)"), in_=b2_bf16[:])
        transpose_z(3, 0, nc.scalar.copy)
        transpose_z(3, 1, nc.scalar.copy)
        regroup_h(1, SHARES)

        for u in range(2, UNITS + 2):
            layer1(u, 0)
            layer2(u - 2, 0)
            layer1(u, 1)
            layer2(u - 2, 1)
            layer1(u, 2)
            layer2(u - 2, 2)
            layer1(u, 3)
            layer2(u - 2, 3)
            transpose_z(u + 2, 0, nc.scalar.copy)
            transpose_z(u + 2, 1, nc.scalar.copy)
            quantise_z(u + 1)
            quantise_h(u - 1)
            for t in range(PACK):
                rows_back(u - 2, t)
                finish(u - 2, t)
                if t == PACK - 1 or u - 2 == UNITS - 1:
                    store(u - 2, t)
            regroup_h(u, SHARES)
